import numpy as np
import ml_dtypes


def mxq(x, axis, fmt="e4m3"):
    dtype, down = {"e4m3": (ml_dtypes.float8_e4m3fn, 7), "e5m2": (ml_dtypes.float8_e5m2, 14)}[fmt]
    v = np.moveaxis(np.asarray(x, np.float32).astype(ml_dtypes.bfloat16).astype(np.float64), axis, -1)
    blocks = v.reshape(v.shape[:-1] + (-1, 32))
    amax = np.abs(blocks).max(-1, keepdims=True)
    byte = np.maximum(np.where(amax > 0, np.frexp(amax)[1] - 1 + 127, 0) - down, 1)
    scale = np.exp2(byte - 127.0)
    codes = (blocks / scale).astype(np.float32).astype(dtype).astype(np.float64)
    return np.moveaxis((codes * scale).reshape(v.shape), -1, axis)


WIDE = False


def mx_kscale(k):
    if not WIDE:
        return np.ones(k)
    levels = np.array([10, -10, 5, -5, 0])
    if k % 512:
        return np.exp2(np.random.permutation(np.resize(levels, k // 32))).repeat(32)
    a = np.empty((k // 512, 16))
    for p in range(k // 512):
        a[p, :8] = np.random.permutation(np.resize(levels, 8))
        for g in range(8):
            far = levels[np.abs(levels - a[p, g]) >= 10]
            a[p, g + 8] = far[np.random.randint(len(far))]
    return np.exp2(a.ravel()).repeat(32)


BF16 = ml_dtypes.bfloat16


def bf(x):
    return np.asarray(x, np.float32).astype(BF16)


def f64(x):
    return np.asarray(x).astype(np.float64)


T, S, B, E, H = 1024, 128, 8, 1024, 512
SCALE = H ** -0.5


def wn_weight(V, g):
    return V * (g / np.linalg.norm(V, axis=1))[:, None]


def draw_wn(rows, cols, gain, kfac, rfac):
    v0 = np.random.standard_normal((rows, cols)) * np.exp(0.5 * np.random.standard_normal((rows, 1))) * 0.5 / np.sqrt(cols)
    v = bf(v0 / kfac)
    g = gain * (1.0 + 0.1 * np.random.standard_normal(rows)) * rfac * np.linalg.norm(f64(v), axis=1) / np.linalg.norm(v0, axis=1)
    return v, bf(g)


def setup_inputs():
    s, t = mx_kscale(E), mx_kscale(H)
    Vq, gq = draw_wn(H, E, 3.2, s, t)
    Vk, gk = draw_wn(H, E, 0.8, s, 1.0 / t)
    return {"query": bf(np.random.standard_normal((T, B, E)) * s), "key": bf(np.random.standard_normal((S, B, E)) * s),
            "Vq": Vq, "gq": gq, "bq": bf(np.random.standard_normal(H) * 0.4 * t),
            "Vk": Vk, "gk": gk, "bk": bf(np.random.standard_normal(H) * 0.1 / t)}


def reference(query, key, Vq, gq, bq, Vk, gk, bk):
    Wq = wn_weight(f64(Vq), f64(gq))
    Wk = wn_weight(f64(Vk), f64(gk))
    q = ((mxq(f64(query), 2, "e4m3") @ mxq(Wq, 1, "e4m3").T) + f64(bq)) * SCALE
    k = (mxq(f64(key), 2, "e4m3") @ mxq(Wk, 1, "e4m3").T) + f64(bk)
    return mxq(q.transpose(1, 0, 2), 2, "e4m3") @ mxq(k.transpose(1, 2, 0), 1, "e4m3")

@@ -1,0 +1,290 @@
+from contextlib import ExitStack
+
+import concourse.mybir as mybir
+from concourse.masks import make_identity
+
+F32 = mybir.dt.float32
+BF16 = mybir.dt.bfloat16
+U32 = mybir.dt.uint32
+U8 = mybir.dt.uint8
+FP8X4 = mybir.dt.float8_e4m3fn_x4
+ALU = mybir.AluOpType
+ACTF = mybir.ActivationFunctionType
+
+T, S, B, E, H = 1024, 128, 8, 1024, 512
+P = 128
+PACK = 4
+PASSES = E // (P * PACK)
+SCALE = H ** -0.5
+FLOPS = 2 * (T * B * E * H + S * B * E * H + B * T * S * H)
+
+UB = 4
+HALVES = B // UB
+UNITS = [("k", h) for h in range(HALVES)] + [("q", i) for i in range((T // P) * HALVES)]
+FIRST_QUERY = HALVES
+AHEAD = 2
+RAW_BUFS = 6
+
+
+def tile_singleheadattention_pa_t_kernel(tc, query, key, Vq, gq, bq, Vk, gk, bk, out):
+    nc = tc.nc
+    with ExitStack() as ctx:
+        const = ctx.enter_context(tc.tile_pool(name="const", bufs=1))
+        rawp = ctx.enter_context(tc.tile_pool(name="rawp", bufs=RAW_BUFS))
+        wgp = ctx.enter_context(tc.tile_pool(name="wgp", bufs=4))
+        xgp = ctx.enter_context(tc.tile_pool(name="xgp", bufs=3))
+        xcp = ctx.enter_context(tc.tile_pool(name="xcp", bufs=AHEAD + 2))
+        qgp = ctx.enter_context(tc.tile_pool(name="qgp", bufs=3))
+        qcp = ctx.enter_context(tc.tile_pool(name="qcp", bufs=3))
+        otp = ctx.enter_context(tc.tile_pool(name="otp", bufs=3))
+        ps_t = ctx.enter_context(tc.psum_pool(name="ps_t", bufs=4))
+        ps_q = ctx.enter_context(tc.psum_pool(name="ps_q", bufs=3))
+        ps_l = ctx.enter_context(tc.psum_pool(name="ps_l", bufs=1))
+        ctx.enter_context(tc.manual_schedule())
+
+        vec = {}
+        for nm, src in (("gk", gk), ("bk", bk), ("gq", gq), ("bq", bq)):
+            vt = const.tile([P, PACK], BF16, name="vec_" + nm)
+            nc.scalar.dma_start(out=vt[:], in_=src.rearrange("(c j) -> c j", j=PACK))
+            vec[nm] = vt
+        warm_in = const.tile([P, 1], F32, name="warm_in")
+        warm_out = const.tile([P, 1], F32, name="warm_out")
+        nc.vector.memset(warm_in[:], 1.0)
+        nc.scalar.sqrt(out=warm_out[:], in_=warm_in[:])
+        ident_b = const.tile([P, P], BF16, name="ident_b")
+        ident_f = const.tile([P, P], F32, name="ident_f")
+        make_identity(nc, ident_b[:])
+        make_identity(nc, ident_f[:])
+
+        v_dram = {"q": Vq, "k": Vk}
+        post_scale = {"q": SCALE, "k": 1.0}
+        v_raw, w_sb, ss_act, ss_dve, norm, rnorm, row_gain, w_codes, w_scales, bias = {}, {}, {}, {}, {}, {}, {}, {}, {}, {}
+        for w in ("k", "q"):
+            v_raw[w] = const.tile([P, PACK * E], BF16, name="v_raw_" + w)
+            w_sb[w] = const.tile([P, PACK * E], BF16, name="w_sb_" + w)
+            ss_act[w] = const.tile([P, PACK], F32, name="ss_act_" + w)
+            ss_dve[w] = const.tile([P, PACK], F32, name="ss_dve_" + w)
+            norm[w] = const.tile([P, PACK], F32, name="norm_" + w)
+            rnorm[w] = const.tile([P, PACK], F32, name="rnorm_" + w)
+            row_gain[w] = const.tile([P, PACK], F32, name="row_gain_" + w)
+            bias[w] = const.tile([P, PACK], F32, name="bias_" + w)
+            w_codes[w] = const.tile([P, PACK * PASSES * P], U32, name="w_codes_" + w, align_bytes=64)
+            w_scales[w] = const.tile([P, PACK * PASSES * P], U8, name="w_scales_" + w, align_bytes=64)
+        squares_act = const.tile([P, E], BF16, name="squares_act")
+        squares_dve = const.tile([P, E], F32, name="squares_dve")
+        k_codes = const.tile([P, B * S], U32, name="k_codes", align_bytes=64)
+        k_scales = const.tile([P, B * S], U8, name="k_scales", align_bytes=64)
+
+        raw, x_grouped, x_codes, x_scales, q_grouped, q_codes, q_scales, w_grouped = {}, {}, {}, {}, {}, {}, {}, {}
+
+        def load_v(w):
+            src = v_dram[w].rearrange("(c j) e -> c j e", j=PACK)
+            for j in range(PACK):
+                nc.sync.dma_start(out=v_raw[w][:, j * E:(j + 1) * E], in_=src[:, j, :])
+
+        def load(n):
+            kind, i = UNITS[n]
+            raw[n] = rawp.tile([P, UB * E], BF16, name="raw")
+            if kind == "k":
+                src = key[:, UB * i:UB * (i + 1), :]
+            else:
+                c, h = divmod(i, HALVES)
+                src = query[P * c:P * (c + 1), UB * h:UB * (h + 1), :]
+            nc.sync.dma_start(out=raw[n][:], in_=src.rearrange("t b e -> t (b e)"))
+
+        def square(w, j):
+            vj = v_raw[w][:, j * E:(j + 1) * E]
+            if j % 2 == 0:
+                nc.scalar.activation(out=squares_act[:], in_=vj, func=ACTF.Square, accum_out=ss_act[w][:, j:j + 1])
+            else:
+                nc.vector.scalar_tensor_tensor(out=squares_dve[:], in0=vj, scalar=1.0, in1=vj, op0=ALU.mult,
+                                               op1=ALU.mult, accum_out=ss_dve[w][:, j:j + 1])
+
+        def scale(w):
+            even, odd = slice(0, PACK, 2), slice(1, PACK, 2)
+            nc.scalar.sqrt(out=norm[w][:, even], in_=ss_act[w][:, even])
+            nc.scalar.sqrt(out=norm[w][:, odd], in_=ss_dve[w][:, odd])
+            nc.vector.reciprocal(out=rnorm[w][:], in_=norm[w][:])
+            nc.vector.tensor_tensor(out=row_gain[w][:], in0=rnorm[w][:], in1=vec["g" + w][:], op=ALU.mult)
+
+        def mult(w, j):
+            cols = slice(j * E, (j + 1) * E)
+            nc.vector.tensor_scalar(out=w_sb[w][:, cols], in0=v_raw[w][:, cols],
+                                    scalar1=row_gain[w][:, j:j + 1], scalar2=None, op0=ALU.mult)
+
+        def w_t(w, j, g, engine):
+            picked = w_sb[w][:].rearrange("c (j g p t) -> c j g t p", j=PACK, g=PASSES, t=PACK)
+            bank = ps_t.tile([P, PACK * P], BF16, name="w_bank", tag="t_bank")
+            for t in range(PACK):
+                nc.tensor.transpose(out=bank[:, t * P:(t + 1) * P], in_=picked[:, j, g, t, :], identity=ident_b[:])
+            if g == 0:
+                w_grouped[(w, j)] = wgp.tile([P, PASSES * P * PACK], BF16, name="w_grouped", align_bytes=64)
+            dst = w_grouped[(w, j)][:, g * P * PACK:(g + 1) * P * PACK].rearrange("p (c t) -> p c t", t=PACK)
+            src = bank[:].rearrange("p (t c) -> p c t", t=PACK)
+            if engine == "act":
+                nc.scalar.copy(out=dst, in_=src)
+            else:
+                nc.vector.tensor_copy(out=dst, in_=src)
+
+        def w_q(w, j):
+            cols = slice(j * PASSES * P, (j + 1) * PASSES * P)
+            nc.vector.quantize_mx(out=w_codes[w][:, cols].bitcast(FP8X4), scales=w_scales[w][:, cols],
+                                  in_=w_grouped[(w, j)][:])
+
+        def bias_prep():
+            nc.vector.tensor_copy(out=bias["k"][:], in_=vec["bk"][:])
+            nc.vector.tensor_scalar(out=bias["q"][:], in0=vec["bq"][:], scalar1=SCALE, scalar2=None, op0=ALU.mult)
+
+        def x_t(n, b):
+            if b == 0:
+                x_grouped[n] = xgp.tile([P, UB * E], BF16, name="x_grouped", align_bytes=64)
+                x_codes[n] = xcp.tile([P, UB * PASSES * P], U32, name="x_codes", align_bytes=64)
+                x_scales[n] = xcp.tile([P, UB * PASSES * P], U8, name="x_scales", align_bytes=64)
+            words_in = raw[n][:].bitcast(F32)
+            words_out = x_grouped[n][:].bitcast(F32)
+            row_words = E // 2
+            bank = ps_t.tile([P, row_words], F32, name="x_bank", tag="t_bank")
+            for g in range(PASSES):
+                for u in range(2):
+                    gu = 2 * g + u
+                    col = b * row_words + g * 2 * P
+                    nc.tensor.transpose(out=bank[:, gu * P:(gu + 1) * P], in_=words_in[:, col + u:col + 2 * P:2],
+                                        identity=ident_f[:])
+            dst = words_out[:, b * row_words:(b + 1) * row_words].rearrange("p (g r u) -> p g r u", g=PASSES, u=2)
+            nc.scalar.copy(out=dst, in_=bank[:].rearrange("p (g u r) -> p g r u", g=PASSES, u=2))
+
+        def x_q(n, b):
+            cols = slice(b * PASSES * P, (b + 1) * PASSES * P)
+            nc.vector.quantize_mx(out=x_codes[n][:, cols].bitcast(FP8X4), scales=x_scales[n][:, cols],
+                                  in_=x_grouped[n][:, b * E:(b + 1) * E])
+
+        def proj(n, b):
+            w = UNITS[n][0]
+            if b == 0:
+                q_grouped[n] = qgp.tile([P, UB * P * PACK], BF16, name="q_grouped", align_bytes=64)
+                if w == "q":
+                    q_codes[n] = qcp.tile([P, UB * P], U32, name="q_codes", align_bytes=64)
+                    q_scales[n] = qcp.tile([P, UB * P], U8, name="q_scales", align_bytes=64)
+            bank = ps_q.tile([P, PACK * P], F32, name="q_bank")
+            for j in range(PACK):
+                for g in range(PASSES):
+                    wcols = slice((j * PASSES + g) * P, (j * PASSES + g + 1) * P)
+                    xcols = slice((b * PASSES + g) * P, (b * PASSES + g + 1) * P)
+                    nc.tensor.matmul_mx(out=bank[:, j * P:(j + 1) * P],
+                                        lhsT=w_codes[w][:, wcols].bitcast(FP8X4), lhsT_scale=w_scales[w][:, wcols],
+                                        rhs=x_codes[n][:, xcols].bitcast(FP8X4), rhs_scale=x_scales[n][:, xcols],
+                                        start=(g == 0), stop=(g == PASSES - 1))
+            nc.vector.scalar_tensor_tensor(
+                out=q_grouped[n][:, b * P * PACK:(b + 1) * P * PACK].rearrange("c (r j) -> c r j", j=PACK),
+                in0=bank[:].rearrange("c (j r) -> c r j", j=PACK), scalar=post_scale[w],
+                in1=bias[w][:].unsqueeze(1).to_broadcast([P, P, PACK]), op0=ALU.mult, op1=ALU.add)
+
+        def q_q(n, half):
+            w, i = UNITS[n]
+            width = UB // 2 * P
+            src = q_grouped[n][:, half * width * PACK:(half + 1) * width * PACK]
+            if w == "k":
+                cols = slice((i * 2 + half) * width, (i * 2 + half + 1) * width)
+                nc.vector.quantize_mx(out=k_codes[:, cols].bitcast(FP8X4), scales=k_scales[:, cols], in_=src)
+            else:
+                cols = slice(half * width, (half + 1) * width)
+                nc.vector.quantize_mx(out=q_codes[n][:, cols].bitcast(FP8X4), scales=q_scales[n][:, cols], in_=src)
+
+        def logits(n):
+            c, h = divmod(UNITS[n][1], HALVES)
+            bank = ps_l.tile([P, UB * S], F32, name="l_bank")
+            for i in range(UB):
+                qcols = slice(i * P, (i + 1) * P)
+                kcols = slice((h * UB + i) * S, (h * UB + i + 1) * S)
+                nc.tensor.matmul_mx(out=bank[:, i * S:(i + 1) * S],
+                                    lhsT=q_codes[n][:, qcols].bitcast(FP8X4), lhsT_scale=q_scales[n][:, qcols],
+                                    rhs=k_codes[:, kcols].bitcast(FP8X4), rhs_scale=k_scales[:, kcols],
+                                    start=True, stop=True)
+            staged = otp.tile([P, UB * S], F32, name="staged")
+            nc.scalar.copy(out=staged[:], in_=bank[:])
+            nc.scalar.dma_start(out=out[UB * h:UB * (h + 1), P * c:P * (c + 1), :].rearrange("b t s -> t b s"),
+                                in_=staged[:].rearrange("t (b s) -> t b s", b=UB))
+
+        def transposes(n):
+            for b in range(UB):
+                x_t(n, b)
+
+        def row_tile(i, b, ahead):
+            if i < n_units:
+                proj(i, b)
+            if i + ahead < n_units:
+                x_q(i + ahead, b)
+            if b == 0 and i > 0:
+                q_q(i - 1, 1)
+            if b == 2 and i < n_units:
+                q_q(i, 0)
+
+        def query_weights(j):
+            w_t("q", j, 0, "act")
+            w_t("q", j, 1, "act")
+            w_q("q", j)
+
+        n_units = len(UNITS)
+        load_v("k")
+        load_v("q")
+        for n in range(RAW_BUFS):
+            load(n)
+
+        for j in range(PACK):
+            square("k", j)
+        scale("k")
+        square("q", 0)
+        for j in range(PACK):
+            mult("k", j)
+        bias_prep()
+        for j in range(PACK):
+            w_t("k", j, 0, "act")
+            w_t("k", j, 1, "dve")
+            if j > 0:
+                w_q("k", j - 1)
+            if j % 2 == 1:
+                square("q", j)
+        square("q", 2)
+        w_q("k", PACK - 1)
+
+        for b in range(UB):
+            x_t(0, b)
+            if b > 0:
+                x_q(0, b - 1)
+        load(RAW_BUFS)
+        x_q(0, UB - 1)
+        scale("q")
+        for j in range(PACK):
+            mult("q", j)
+        transposes(1)
+        load(RAW_BUFS + 1)
+
+        row_tile(0, 0, 1)
+        row_tile(0, 1, 1)
+        transposes(2)
+        row_tile(0, 2, 1)
+        row_tile(0, 3, 1)
+        query_weights(0)
+        query_weights(1)
+        load(RAW_BUFS + 2)
+        row_tile(1, 0, 1)
+        row_tile(1, 1, 1)
+        query_weights(2)
+        query_weights(3)
+        row_tile(1, 2, 1)
+        row_tile(1, 3, 1)
+        transposes(3)
+        load(RAW_BUFS + 3)
+
+        for i in range(FIRST_QUERY, n_units + 1):
+            if i + AHEAD < n_units:
+                transposes(i + AHEAD)
+            if i + AHEAD + RAW_BUFS < n_units:
+                load(i + AHEAD + RAW_BUFS)
+            if i == FIRST_QUERY:
+                for b in range(UB):
+                    x_q(i + 1, b)
+            for b in range(UB):
+                row_tile(i, b, AHEAD)
+            if i - 1 >= FIRST_QUERY:
+                logits(i - 1)

@@ -22,6 +22,7 @@ UB = 4
 HALVES = B // UB
 UNITS = [("k", h) for h in range(HALVES)] + [("q", i) for i in range((T // P) * HALVES)]
 FIRST_QUERY = HALVES
+SORTED = 3
 AHEAD = 2
 RAW_BUFS = 6
 
@@ -36,6 +37,7 @@ def tile_singleheadattention_pa_t_kernel(tc, query, key, Vq, gq, bq, Vk, gk, bk,
         xcp = ctx.enter_context(tc.tile_pool(name="xcp", bufs=AHEAD + 2))
         qgp = ctx.enter_context(tc.tile_pool(name="qgp", bufs=3))
         qcp = ctx.enter_context(tc.tile_pool(name="qcp", bufs=3))
+        xpp = ctx.enter_context(tc.tile_pool(name="xpp", bufs=3))
         otp = ctx.enter_context(tc.tile_pool(name="otp", bufs=3))
         ps_t = ctx.enter_context(tc.psum_pool(name="ps_t", bufs=4))
         ps_q = ctx.enter_context(tc.psum_pool(name="ps_q", bufs=3))
@@ -75,7 +77,7 @@ def tile_singleheadattention_pa_t_kernel(tc, query, key, Vq, gq, bq, Vk, gk, bk,
         k_codes = const.tile([P, B * S], U32, name="k_codes", align_bytes=64)
         k_scales = const.tile([P, B * S], U8, name="k_scales", align_bytes=64)
 
-        raw, x_grouped, x_codes, x_scales, q_grouped, q_codes, q_scales, w_grouped = {}, {}, {}, {}, {}, {}, {}, {}
+        raw, x_sorted, x_grouped, x_codes, x_scales, q_grouped, q_codes, q_scales, w_grouped = {}, {}, {}, {}, {}, {}, {}, {}, {}
 
         def load_v(w):
             src = v_dram[w].rearrange("(c j) e -> c j e", j=PACK)
@@ -135,6 +137,13 @@ def tile_singleheadattention_pa_t_kernel(tc, query, key, Vq, gq, bq, Vk, gk, bk,
             nc.vector.tensor_copy(out=bias["k"][:], in_=vec["bk"][:])
             nc.vector.tensor_scalar(out=bias["q"][:], in0=vec["bq"][:], scalar1=SCALE, scalar2=None, op0=ALU.mult)
 
+        def sort_words(n, b):
+            if b == 0:
+                x_sorted[n] = xpp.tile([P, SORTED * (E // 2)], F32, name="x_sorted")
+            cols = slice(b * (E // 2), (b + 1) * (E // 2))
+            nc.scalar.copy(out=x_sorted[n][:, cols].rearrange("p (u q) -> p u q", u=2),
+                           in_=raw[n][:].bitcast(F32)[:, cols].rearrange("p (q u) -> p u q", u=2))
+
         def x_t(n, b):
             if b == 0:
                 x_grouped[n] = xgp.tile([P, UB * E], BF16, name="x_grouped", align_bytes=64)
@@ -147,9 +156,13 @@ def tile_singleheadattention_pa_t_kernel(tc, query, key, Vq, gq, bq, Vk, gk, bk,
             for g in range(PASSES):
                 for u in range(2):
                     gu = 2 * g + u
-                    col = b * row_words + g * 2 * P
-                    nc.tensor.transpose(out=bank[:, gu * P:(gu + 1) * P], in_=words_in[:, col + u:col + 2 * P:2],
-                                        identity=ident_f[:])
+                    if n in x_sorted and b < SORTED:
+                        col = b * row_words + u * (row_words // 2) + g * P
+                        picked = x_sorted[n][:, col:col + P]
+                    else:
+                        col = b * row_words + g * 2 * P
+                        picked = words_in[:, col + u:col + 2 * P:2]
+                    nc.tensor.transpose(out=bank[:, gu * P:(gu + 1) * P], in_=picked, identity=ident_f[:])
             dst = words_out[:, b * row_words:(b + 1) * row_words].rearrange("p (g r u) -> p g r u", g=PASSES, u=2)
             nc.scalar.copy(out=dst, in_=bank[:].rearrange("p (g u r) -> p g r u", g=PASSES, u=2))
 
@@ -279,6 +292,9 @@ def tile_singleheadattention_pa_t_kernel(tc, query, key, Vq, gq, bq, Vk, gk, bk,
         for i in range(FIRST_QUERY, n_units + 1):
             if i + AHEAD < n_units:
                 transposes(i + AHEAD)
+                if i + AHEAD + 1 < n_units:
+                    for b in range(SORTED):
+                        sort_words(i + AHEAD + 1, b)
             if i + AHEAD + RAW_BUFS < n_units:
                 load(i + AHEAD + RAW_BUFS)
             if i == FIRST_QUERY:

@@ -22,7 +22,7 @@ UB = 4
 HALVES = B // UB
 UNITS = [("k", h) for h in range(HALVES)] + [("q", i) for i in range((T // P) * HALVES)]
 FIRST_QUERY = HALVES
-SORTED = 3
+SORTED = 2
 AHEAD = 2
 RAW_BUFS = 6
 
@@ -137,12 +137,11 @@ def tile_singleheadattention_pa_t_kernel(tc, query, key, Vq, gq, bq, Vk, gk, bk,
             nc.vector.tensor_copy(out=bias["k"][:], in_=vec["bk"][:])
             nc.vector.tensor_scalar(out=bias["q"][:], in0=vec["bq"][:], scalar1=SCALE, scalar2=None, op0=ALU.mult)
 
-        def sort_words(n, b):
-            if b == 0:
-                x_sorted[n] = xpp.tile([P, SORTED * (E // 2)], F32, name="x_sorted")
-            cols = slice(b * (E // 2), (b + 1) * (E // 2))
-            nc.scalar.copy(out=x_sorted[n][:, cols].rearrange("p (u q) -> p u q", u=2),
-                           in_=raw[n][:].bitcast(F32)[:, cols].rearrange("p (q u) -> p u q", u=2))
+        def sort_words(n):
+            width = SORTED * (E // 2)
+            x_sorted[n] = xpp.tile([P, width], F32, name="x_sorted")
+            nc.scalar.copy(out=x_sorted[n][:].rearrange("p (u q) -> p u q", u=2),
+                           in_=raw[n][:].bitcast(F32)[:, :width].rearrange("p (q u) -> p u q", u=2))
 
         def x_t(n, b):
             if b == 0:
@@ -157,7 +156,7 @@ def tile_singleheadattention_pa_t_kernel(tc, query, key, Vq, gq, bq, Vk, gk, bk,
                 for u in range(2):
                     gu = 2 * g + u
                     if n in x_sorted and b < SORTED:
-                        col = b * row_words + u * (row_words // 2) + g * P
+                        col = (u * SORTED + b) * (row_words // 2) + g * P
                         picked = x_sorted[n][:, col:col + P]
                     else:
                         col = b * row_words + g * 2 * P
@@ -293,8 +292,7 @@ def tile_singleheadattention_pa_t_kernel(tc, query, key, Vq, gq, bq, Vk, gk, bk,
             if i + AHEAD < n_units:
                 transposes(i + AHEAD)
                 if i + AHEAD + 1 < n_units:
-                    for b in range(SORTED):
-                        sort_words(i + AHEAD + 1, b)
+                    sort_words(i + AHEAD + 1)
             if i + AHEAD + RAW_BUFS < n_units:
                 load(i + AHEAD + RAW_BUFS)
             if i == FIRST_QUERY:

@@ -23,6 +23,7 @@ HALVES = B // UB
 UNITS = [("k", h) for h in range(HALVES)] + [("q", i) for i in range((T // P) * HALVES)]
 FIRST_QUERY = HALVES
 SORTED = 2
+RUN = 2
 AHEAD = 2
 RAW_BUFS = 6
 
@@ -289,16 +290,17 @@ def tile_singleheadattention_pa_t_kernel(tc, query, key, Vq, gq, bq, Vk, gk, bk,
         load(RAW_BUFS + 3)
 
         for i in range(FIRST_QUERY, n_units + 1):
-            if i + AHEAD < n_units:
-                transposes(i + AHEAD)
-                if i + AHEAD + 1 < n_units:
-                    sort_words(i + AHEAD + 1)
-            if i + AHEAD + RAW_BUFS < n_units:
-                load(i + AHEAD + RAW_BUFS)
             if i == FIRST_QUERY:
                 for b in range(UB):
                     x_q(i + 1, b)
             for b in range(UB):
+                if b % RUN == 0 and i + AHEAD < n_units:
+                    for ahead_b in range(b, b + RUN):
+                        x_t(i + AHEAD, ahead_b)
+                    if b == 0 and i + AHEAD + 1 < n_units:
+                        sort_words(i + AHEAD + 1)
                 row_tile(i, b, AHEAD)
+            if i + AHEAD + RAW_BUFS < n_units:
+                load(i + AHEAD + RAW_BUFS)
             if i - 1 >= FIRST_QUERY:
                 logits(i - 1)

@@ -20,11 +20,16 @@ FLOPS = 2 * (T * B * E * H + S * B * E * H + B * T * S * H)
 
 UB = 4
 HALVES = B // UB
-UNITS = [("k", h) for h in range(HALVES)] + [("q", i) for i in range((T // P) * HALVES)]
-FIRST_QUERY = HALVES
+KEY_AT = 6
+QUERIES = [("q", i) for i in range((T // P) * HALVES)]
+UNITS = QUERIES[:KEY_AT] + [("k", h) for h in range(HALVES)] + QUERIES[KEY_AT:]
 SORTED = 2
+SORTED_VECTOR = 1
+FIRST_SORT = 2
+ON_SCALAR = {"q": (0, 2,), "k": (0, 1, 2, 3,)}
 RUN = 2
-AHEAD = 2
+T_AHEAD = 8
+Q_AHEAD = 6
 RAW_BUFS = 6
 
 
@@ -35,14 +40,13 @@ def tile_singleheadattention_pa_t_kernel(tc, query, key, Vq, gq, bq, Vk, gk, bk,
         rawp = ctx.enter_context(tc.tile_pool(name="rawp", bufs=RAW_BUFS))
         wgp = ctx.enter_context(tc.tile_pool(name="wgp", bufs=4))
         xgp = ctx.enter_context(tc.tile_pool(name="xgp", bufs=3))
-        xcp = ctx.enter_context(tc.tile_pool(name="xcp", bufs=AHEAD + 2))
+        xcp = ctx.enter_context(tc.tile_pool(name="xcp", bufs=3))
         qgp = ctx.enter_context(tc.tile_pool(name="qgp", bufs=3))
-        qcp = ctx.enter_context(tc.tile_pool(name="qcp", bufs=3))
+        qcp = ctx.enter_context(tc.tile_pool(name="qcp", bufs=KEY_AT + 5))
         xpp = ctx.enter_context(tc.tile_pool(name="xpp", bufs=3))
         otp = ctx.enter_context(tc.tile_pool(name="otp", bufs=3))
         ps_t = ctx.enter_context(tc.psum_pool(name="ps_t", bufs=4))
-        ps_q = ctx.enter_context(tc.psum_pool(name="ps_q", bufs=3))
-        ps_l = ctx.enter_context(tc.psum_pool(name="ps_l", bufs=1))
+        ps_q = ctx.enter_context(tc.psum_pool(name="ps_q", bufs=4))
         ctx.enter_context(tc.manual_schedule())
 
         vec = {}
@@ -59,6 +63,14 @@ def tile_singleheadattention_pa_t_kernel(tc, query, key, Vq, gq, bq, Vk, gk, bk,
         make_identity(nc, ident_b[:])
         make_identity(nc, ident_f[:])
 
+        warm_rhs = const.tile([P, PACK * P], BF16, name="warm_rhs")
+        nc.vector.memset(warm_rhs[:], 0.0)
+
+        def warm(count):
+            bank = ps_q.tile([P, PACK * P], F32, name="warm_bank", tag="q_bank")
+            for m in range(count):
+                nc.tensor.matmul(out=bank[:], lhsT=ident_b[:], rhs=warm_rhs[:], start=True, stop=True)
+
         v_dram = {"q": Vq, "k": Vk}
         post_scale = {"q": SCALE, "k": 1.0}
         v_raw, w_sb, ss_act, ss_dve, norm, rnorm, row_gain, w_codes, w_scales, bias = {}, {}, {}, {}, {}, {}, {}, {}, {}, {}
@@ -74,7 +86,7 @@ def tile_singleheadattention_pa_t_kernel(tc, query, key, Vq, gq, bq, Vk, gk, bk,
             w_codes[w] = const.tile([P, PACK * PASSES * P], U32, name="w_codes_" + w, align_bytes=64)
             w_scales[w] = const.tile([P, PACK * PASSES * P], U8, name="w_scales_" + w, align_bytes=64)
         squares_act = const.tile([P, E], BF16, name="squares_act")
-        squares_dve = const.tile([P, E], F32, name="squares_dve")
+        squares_dve = const.tile([P, E], BF16, name="squares_dve")
         k_codes = const.tile([P, B * S], U32, name="k_codes", align_bytes=64)
         k_scales = const.tile([P, B * S], U8, name="k_scales", align_bytes=64)
 
@@ -93,20 +105,31 @@ def tile_singleheadattention_pa_t_kernel(tc, query, key, Vq, gq, bq, Vk, gk, bk,
             else:
                 c, h = divmod(i, HALVES)
                 src = query[P * c:P * (c + 1), UB * h:UB * (h + 1), :]
-            nc.sync.dma_start(out=raw[n][:], in_=src.rearrange("t b e -> t (b e)"))
+            pieces = UB if n == 0 else 1
+            width = UB // pieces
+            for m in range(pieces):
+                nc.sync.dma_start(out=raw[n][:, m * width * E:(m + 1) * width * E],
+                                  in_=src[:, m * width:(m + 1) * width, :].rearrange("t b e -> t (b e)"))
+
+        def on_scalar(w, j):
+            return j in ON_SCALAR[w]
 
         def square(w, j):
             vj = v_raw[w][:, j * E:(j + 1) * E]
-            if j % 2 == 0:
+            if on_scalar(w, j):
                 nc.scalar.activation(out=squares_act[:], in_=vj, func=ACTF.Square, accum_out=ss_act[w][:, j:j + 1])
             else:
                 nc.vector.scalar_tensor_tensor(out=squares_dve[:], in0=vj, scalar=1.0, in1=vj, op0=ALU.mult,
                                                op1=ALU.mult, accum_out=ss_dve[w][:, j:j + 1])
 
         def scale(w):
-            even, odd = slice(0, PACK, 2), slice(1, PACK, 2)
-            nc.scalar.sqrt(out=norm[w][:, even], in_=ss_act[w][:, even])
-            nc.scalar.sqrt(out=norm[w][:, odd], in_=ss_dve[w][:, odd])
+            for j in range(PACK):
+                src = ss_act if on_scalar(w, j) else ss_dve
+                if w == "k" and len(ON_SCALAR[w]) == PACK:
+                    if j == 0:
+                        nc.scalar.sqrt(out=norm[w][:], in_=src[w][:])
+                else:
+                    nc.scalar.sqrt(out=norm[w][:, j:j + 1], in_=src[w][:, j:j + 1])
             nc.vector.reciprocal(out=rnorm[w][:], in_=norm[w][:])
             nc.vector.tensor_tensor(out=row_gain[w][:], in0=rnorm[w][:], in1=vec["g" + w][:], op=ALU.mult)
 
@@ -115,15 +138,20 @@ def tile_singleheadattention_pa_t_kernel(tc, query, key, Vq, gq, bq, Vk, gk, bk,
             nc.vector.tensor_scalar(out=w_sb[w][:, cols], in0=v_raw[w][:, cols],
                                     scalar1=row_gain[w][:, j:j + 1], scalar2=None, op0=ALU.mult)
 
-        def w_t(w, j, g, engine):
-            picked = w_sb[w][:].rearrange("c (j g p t) -> c j g t p", j=PACK, g=PASSES, t=PACK)
-            bank = ps_t.tile([P, PACK * P], BF16, name="w_bank", tag="t_bank")
-            for t in range(PACK):
-                nc.tensor.transpose(out=bank[:, t * P:(t + 1) * P], in_=picked[:, j, g, t, :], identity=ident_b[:])
-            if g == 0:
-                w_grouped[(w, j)] = wgp.tile([P, PASSES * P * PACK], BF16, name="w_grouped", align_bytes=64)
-            dst = w_grouped[(w, j)][:, g * P * PACK:(g + 1) * P * PACK].rearrange("p (c t) -> p c t", t=PACK)
-            src = bank[:].rearrange("p (t c) -> p c t", t=PACK)
+        def w_t(w, j, engine):
+            w_grouped[(w, j)] = wgp.tile([P, E], BF16, name="w_grouped", align_bytes=64)
+            words_in = w_sb[w][:].bitcast(F32)
+            words_out = w_grouped[(w, j)][:].bitcast(F32)
+            row_words = E // 2
+            bank = ps_t.tile([P, row_words], F32, name="w_bank", tag="t_bank")
+            for g in range(PASSES):
+                for u in range(2):
+                    gu = 2 * g + u
+                    col = j * row_words + g * 2 * P
+                    nc.tensor.transpose(out=bank[:, gu * P:(gu + 1) * P], in_=words_in[:, col + u:col + 2 * P:2],
+                                        identity=ident_f[:])
+            dst = words_out.rearrange("p (g c u) -> p g c u", g=PASSES, u=2)
+            src = bank[:].rearrange("p (g u c) -> p g c u", g=PASSES, u=2)
             if engine == "act":
                 nc.scalar.copy(out=dst, in_=src)
             else:
@@ -138,17 +166,23 @@ def tile_singleheadattention_pa_t_kernel(tc, query, key, Vq, gq, bq, Vk, gk, bk,
             nc.vector.tensor_copy(out=bias["k"][:], in_=vec["bk"][:])
             nc.vector.tensor_scalar(out=bias["q"][:], in0=vec["bq"][:], scalar1=SCALE, scalar2=None, op0=ALU.mult)
 
-        def sort_words(n):
-            width = SORTED * (E // 2)
-            x_sorted[n] = xpp.tile([P, width], F32, name="x_sorted")
-            nc.scalar.copy(out=x_sorted[n][:].rearrange("p (u q) -> p u q", u=2),
-                           in_=raw[n][:].bitcast(F32)[:, :width].rearrange("p (q u) -> p u q", u=2))
+        def sort_words(n, engine):
+            if n not in x_sorted:
+                x_sorted[n] = xpp.tile([P, UB * (E // 2)], F32, name="x_sorted")
+            words = raw[n][:].bitcast(F32)
+            if engine == "act":
+                cols = slice(0, SORTED * (E // 2))
+                nc.scalar.copy(out=x_sorted[n][:, cols].rearrange("p (u q) -> p u q", u=2),
+                               in_=words[:, cols].rearrange("p (q u) -> p u q", u=2))
+            else:
+                for b in range(SORTED, SORTED + SORTED_VECTOR):
+                    cols = slice(b * (E // 2), (b + 1) * (E // 2))
+                    nc.vector.tensor_copy(out=x_sorted[n][:, cols].rearrange("p (u q) -> p u q", u=2),
+                                          in_=words[:, cols].rearrange("p (q u) -> p u q", u=2))
 
         def x_t(n, b):
             if b == 0:
                 x_grouped[n] = xgp.tile([P, UB * E], BF16, name="x_grouped", align_bytes=64)
-                x_codes[n] = xcp.tile([P, UB * PASSES * P], U32, name="x_codes", align_bytes=64)
-                x_scales[n] = xcp.tile([P, UB * PASSES * P], U8, name="x_scales", align_bytes=64)
             words_in = raw[n][:].bitcast(F32)
             words_out = x_grouped[n][:].bitcast(F32)
             row_words = E // 2
@@ -156,8 +190,9 @@ def tile_singleheadattention_pa_t_kernel(tc, query, key, Vq, gq, bq, Vk, gk, bk,
             for g in range(PASSES):
                 for u in range(2):
                     gu = 2 * g + u
-                    if n in x_sorted and b < SORTED:
-                        col = (u * SORTED + b) * (row_words // 2) + g * P
+                    if n in x_sorted and b < SORTED + SORTED_VECTOR:
+                        col = (u * SORTED + b) * (row_words // 2) if b < SORTED else (2 * b + u) * (row_words // 2)
+                        col += g * P
                         picked = x_sorted[n][:, col:col + P]
                     else:
                         col = b * row_words + g * 2 * P
@@ -166,10 +201,13 @@ def tile_singleheadattention_pa_t_kernel(tc, query, key, Vq, gq, bq, Vk, gk, bk,
             dst = words_out[:, b * row_words:(b + 1) * row_words].rearrange("p (g r u) -> p g r u", g=PASSES, u=2)
             nc.scalar.copy(out=dst, in_=bank[:].rearrange("p (g u r) -> p g r u", g=PASSES, u=2))
 
-        def x_q(n, b):
-            cols = slice(b * PASSES * P, (b + 1) * PASSES * P)
+        def x_q(n, b, count):
+            if b == 0:
+                x_codes[n] = xcp.tile([P, UB * PASSES * P], U32, name="x_codes", align_bytes=64)
+                x_scales[n] = xcp.tile([P, UB * PASSES * P], U8, name="x_scales", align_bytes=64)
+            cols = slice(b * PASSES * P, (b + count) * PASSES * P)
             nc.vector.quantize_mx(out=x_codes[n][:, cols].bitcast(FP8X4), scales=x_scales[n][:, cols],
-                                  in_=x_grouped[n][:, b * E:(b + 1) * E])
+                                  in_=x_grouped[n][:, b * E:(b + count) * E])
 
         def proj(n, b):
             w = UNITS[n][0]
@@ -178,7 +216,7 @@ def tile_singleheadattention_pa_t_kernel(tc, query, key, Vq, gq, bq, Vk, gk, bk,
                 if w == "q":
                     q_codes[n] = qcp.tile([P, UB * P], U32, name="q_codes", align_bytes=64)
                     q_scales[n] = qcp.tile([P, UB * P], U8, name="q_scales", align_bytes=64)
-            bank = ps_q.tile([P, PACK * P], F32, name="q_bank")
+            bank = ps_q.tile([P, PACK * P], F32, name="q_bank", tag="q_bank")
             for j in range(PACK):
                 for g in range(PASSES):
                     wcols = slice((j * PASSES + g) * P, (j * PASSES + g + 1) * P)
@@ -192,115 +230,104 @@ def tile_singleheadattention_pa_t_kernel(tc, query, key, Vq, gq, bq, Vk, gk, bk,
                 in0=bank[:].rearrange("c (j r) -> c r j", j=PACK), scalar=post_scale[w],
                 in1=bias[w][:].unsqueeze(1).to_broadcast([P, P, PACK]), op0=ALU.mult, op1=ALU.add)
 
-        def q_q(n, half):
+        def q_q(n, first, count):
             w, i = UNITS[n]
-            width = UB // 2 * P
-            src = q_grouped[n][:, half * width * PACK:(half + 1) * width * PACK]
+            src = q_grouped[n][:, first * P * PACK:(first + count) * P * PACK]
             if w == "k":
-                cols = slice((i * 2 + half) * width, (i * 2 + half + 1) * width)
+                cols = slice((i * UB + first) * P, (i * UB + first + count) * P)
                 nc.vector.quantize_mx(out=k_codes[:, cols].bitcast(FP8X4), scales=k_scales[:, cols], in_=src)
             else:
-                cols = slice(half * width, (half + 1) * width)
+                cols = slice(first * P, (first + count) * P)
                 nc.vector.quantize_mx(out=q_codes[n][:, cols].bitcast(FP8X4), scales=q_scales[n][:, cols], in_=src)
 
-        def logits(n):
+        def logits(n, first, count):
             c, h = divmod(UNITS[n][1], HALVES)
-            bank = ps_l.tile([P, UB * S], F32, name="l_bank")
-            for i in range(UB):
-                qcols = slice(i * P, (i + 1) * P)
-                kcols = slice((h * UB + i) * S, (h * UB + i + 1) * S)
-                nc.tensor.matmul_mx(out=bank[:, i * S:(i + 1) * S],
+            bank = ps_q.tile([P, UB * S], F32, name="l_bank", tag="q_bank")
+            for m in range(count):
+                qcols = slice((first + m) * P, (first + m + 1) * P)
+                kcols = slice((h * UB + first + m) * S, (h * UB + first + m + 1) * S)
+                nc.tensor.matmul_mx(out=bank[:, m * S:(m + 1) * S],
                                     lhsT=q_codes[n][:, qcols].bitcast(FP8X4), lhsT_scale=q_scales[n][:, qcols],
                                     rhs=k_codes[:, kcols].bitcast(FP8X4), rhs_scale=k_scales[:, kcols],
                                     start=True, stop=True)
             staged = otp.tile([P, UB * S], F32, name="staged")
-            nc.scalar.copy(out=staged[:], in_=bank[:])
-            nc.scalar.dma_start(out=out[UB * h:UB * (h + 1), P * c:P * (c + 1), :].rearrange("b t s -> t b s"),
-                                in_=staged[:].rearrange("t (b s) -> t b s", b=UB))
-
-        def transposes(n):
-            for b in range(UB):
-                x_t(n, b)
-
-        def row_tile(i, b, ahead):
-            if i < n_units:
-                proj(i, b)
-            if i + ahead < n_units:
-                x_q(i + ahead, b)
-            if b == 0 and i > 0:
-                q_q(i - 1, 1)
-            if b == 2 and i < n_units:
-                q_q(i, 0)
-
-        def query_weights(j):
-            w_t("q", j, 0, "act")
-            w_t("q", j, 1, "act")
-            w_q("q", j)
+            nc.scalar.copy(out=staged[:, :count * S], in_=bank[:, :count * S])
+            batches = slice(UB * h + first, UB * h + first + count)
+            nc.sync.dma_start(out=out[batches, P * c:P * (c + 1), :].rearrange("b t s -> t b s"),
+                                in_=staged[:, :count * S].rearrange("t (b s) -> t b s", b=count))
 
         n_units = len(UNITS)
-        load_v("k")
+        n_tiles = n_units * UB
+        done = {"t": 0, "q": 0}
+
+        def tile_t(count):
+            for m in range(count):
+                if done["t"] < n_tiles:
+                    n, b = divmod(done["t"], UB)
+                    x_t(n, b)
+                    done["t"] += 1
+                    if b == UB - 1 and n + RAW_BUFS < n_units:
+                        load(n + RAW_BUFS)
+
+        def tile_q(count):
+            if done["q"] < n_tiles:
+                x_q(done["q"] // UB, done["q"] % UB, count)
+                done["q"] += count
+
         load_v("q")
-        for n in range(RAW_BUFS):
+        load(0)
+        load(1)
+        load_v("k")
+        for n in range(2, RAW_BUFS):
             load(n)
-
+        warm(8)
+        tile_t(0)
         for j in range(PACK):
-            square("k", j)
-        scale("k")
-        square("q", 0)
-        for j in range(PACK):
-            mult("k", j)
+            square("q", j)
         bias_prep()
-        for j in range(PACK):
-            w_t("k", j, 0, "act")
-            w_t("k", j, 1, "dve")
-            if j > 0:
-                w_q("k", j - 1)
-            if j % 2 == 1:
-                square("q", j)
-        square("q", 2)
-        w_q("k", PACK - 1)
-
-        for b in range(UB):
-            x_t(0, b)
-            if b > 0:
-                x_q(0, b - 1)
-        load(RAW_BUFS)
-        x_q(0, UB - 1)
         scale("q")
+        tile_t(2)
         for j in range(PACK):
             mult("q", j)
-        transposes(1)
-        load(RAW_BUFS + 1)
-
-        row_tile(0, 0, 1)
-        row_tile(0, 1, 1)
-        transposes(2)
-        row_tile(0, 2, 1)
-        row_tile(0, 3, 1)
-        query_weights(0)
-        query_weights(1)
-        load(RAW_BUFS + 2)
-        row_tile(1, 0, 1)
-        row_tile(1, 1, 1)
-        query_weights(2)
-        query_weights(3)
-        row_tile(1, 2, 1)
-        row_tile(1, 3, 1)
-        transposes(3)
-        load(RAW_BUFS + 3)
-
-        for i in range(FIRST_QUERY, n_units + 1):
-            if i == FIRST_QUERY:
-                for b in range(UB):
-                    x_q(i + 1, b)
+        for j in range(PACK):
+            w_t("q", j, ("act", "dve")[j % 2])
+            if j > 0:
+                w_q("q", j - 1)
+        tile_q(2)
+        w_q("q", PACK - 1)
+        tile_t(2)
+        key_steps = {1: [lambda: square("k", 0)], 3: [lambda: square("k", 1)], 5: [lambda: square("k", 2)], 7: [lambda: square("k", 3)], 9: [lambda: scale("k")], 10: [lambda: mult("k", 0)], 11: [lambda: mult("k", 1)], 12: [lambda: mult("k", 2)], 13: [lambda: mult("k", 3)], 14: [lambda: w_t("k", 0, "act"), lambda: w_t("k", 1, "act")], 16: [lambda: w_q("k", 0)], 17: [lambda: w_q("k", 1)], 18: [lambda: w_t("k", 2, "act"), lambda: w_t("k", 3, "act")], 20: [lambda: w_q("k", 2)], 21: [lambda: w_q("k", 3)]}
+        waiting = []
+        for i in range(n_units + 1):
+            if 0 < i < n_units and UNITS[i - 1][0] == "q":
+                waiting.append(i - 1)
             for b in range(UB):
-                if b % RUN == 0 and i + AHEAD < n_units:
-                    for ahead_b in range(b, b + RUN):
-                        x_t(i + AHEAD, ahead_b)
-                    if b == 0 and i + AHEAD + 1 < n_units:
-                        sort_words(i + AHEAD + 1)
-                row_tile(i, b, AHEAD)
-            if i + AHEAD + RAW_BUFS < n_units:
-                load(i + AHEAD + RAW_BUFS)
-            if i - 1 >= FIRST_QUERY:
-                logits(i - 1)
+                s = UB * i + b
+                if b % RUN == 0:
+                    tile_t(RUN)
+                    if s // RUN % 2 == 2 - 1 and done["t"] < s + RUN + T_AHEAD:
+                        tile_t(RUN)
+                n = -(-done["t"] // UB)
+                if b == 1 and FIRST_SORT <= i and n < n_units and SORTED:
+                    sort_words(n, "act")
+                for step in key_steps.get(s, []):
+                    step()
+                if i < n_units:
+                    proj(i, b)
+                if b == 1 and FIRST_SORT <= i and n < n_units and SORTED_VECTOR:
+                    sort_words(n, "dve")
+                if b % 2 == 0:
+                    tile_q(2)
+                    if s % 4 == 4 - 2 and done["q"] < s + 2 + Q_AHEAD:
+                        tile_q(2)
+                elif i < n_units or b < 2:
+                    if b == 1 and i > 0:
+                        q_q(i - 1, 2, 2)
+                    if b == 3:
+                        q_q(i, 0, 2)
+                if i >= KEY_AT + HALVES and i < n_units and (b == 3 or b == 1 and len(waiting) > 1) and waiting:
+                    logits(waiting.pop(0), 0, UB)
+        for n in waiting:
+            logits(n, 0, UB)
+        logits(n_units - 1, 0, 2)
+        logits(n_units - 1, 2, 2)

@@ -25,7 +25,7 @@ QUERIES = [("q", i) for i in range((T // P) * HALVES)]
 UNITS = QUERIES[:KEY_AT] + [("k", h) for h in range(HALVES)] + QUERIES[KEY_AT:]
 SORTED = 2
 SORTED_VECTOR = 1
-FIRST_SORT = 2
+FIRST_SORT = 3
 ON_SCALAR = {"q": (0, 2,), "k": (0, 1, 2, 3,)}
 RUN = 2
 T_AHEAD = 8
@@ -57,7 +57,7 @@ def tile_singleheadattention_pa_t_kernel(tc, query, key, Vq, gq, bq, Vk, gk, bk,
         warm_in = const.tile([P, 1], F32, name="warm_in")
         warm_out = const.tile([P, 1], F32, name="warm_out")
         nc.vector.memset(warm_in[:], 1.0)
-        nc.scalar.sqrt(out=warm_out[:], in_=warm_in[:])
+        nc.scalar.activation(out=warm_out[:], in_=warm_in[:], func=ACTF.Abs_reciprocal_sqrt)
         ident_b = const.tile([P, P], BF16, name="ident_b")
         ident_f = const.tile([P, P], F32, name="ident_f")
         make_identity(nc, ident_b[:])
@@ -73,15 +73,14 @@ def tile_singleheadattention_pa_t_kernel(tc, query, key, Vq, gq, bq, Vk, gk, bk,
 
         v_dram = {"q": Vq, "k": Vk}
         post_scale = {"q": SCALE, "k": 1.0}
-        v_raw, w_sb, ss_act, ss_dve, norm, rnorm, row_gain, w_codes, w_scales, bias = {}, {}, {}, {}, {}, {}, {}, {}, {}, {}
+        v_raw, w_sb, ss_act, ss_dve, rnorm, gain, w_codes, w_scales, bias = {}, {}, {}, {}, {}, {}, {}, {}, {}
         for w in ("k", "q"):
             v_raw[w] = const.tile([P, PACK * E], BF16, name="v_raw_" + w)
             w_sb[w] = const.tile([P, PACK * E], BF16, name="w_sb_" + w)
             ss_act[w] = const.tile([P, PACK], F32, name="ss_act_" + w)
             ss_dve[w] = const.tile([P, PACK], F32, name="ss_dve_" + w)
-            norm[w] = const.tile([P, PACK], F32, name="norm_" + w)
             rnorm[w] = const.tile([P, PACK], F32, name="rnorm_" + w)
-            row_gain[w] = const.tile([P, PACK], F32, name="row_gain_" + w)
+            gain[w] = const.tile([P, PACK], F32, name="gain_" + w)
             bias[w] = const.tile([P, PACK], F32, name="bias_" + w)
             w_codes[w] = const.tile([P, PACK * PASSES * P], U32, name="w_codes_" + w, align_bytes=64)
             w_scales[w] = const.tile([P, PACK * PASSES * P], U8, name="w_scales_" + w, align_bytes=64)
@@ -90,6 +89,7 @@ def tile_singleheadattention_pa_t_kernel(tc, query, key, Vq, gq, bq, Vk, gk, bk,
         k_codes = const.tile([P, B * S], U32, name="k_codes", align_bytes=64)
         k_scales = const.tile([P, B * S], U8, name="k_scales", align_bytes=64)
 
+        plane = {}
         raw, x_sorted, x_grouped, x_codes, x_scales, q_grouped, q_codes, q_scales, w_grouped = {}, {}, {}, {}, {}, {}, {}, {}, {}
 
         def load_v(w):
@@ -122,21 +122,14 @@ def tile_singleheadattention_pa_t_kernel(tc, query, key, Vq, gq, bq, Vk, gk, bk,
                 nc.vector.scalar_tensor_tensor(out=squares_dve[:], in0=vj, scalar=1.0, in1=vj, op0=ALU.mult,
                                                op1=ALU.mult, accum_out=ss_dve[w][:, j:j + 1])
 
-        def scale(w):
-            for j in range(PACK):
-                src = ss_act if on_scalar(w, j) else ss_dve
-                if w == "k" and len(ON_SCALAR[w]) == PACK:
-                    if j == 0:
-                        nc.scalar.sqrt(out=norm[w][:], in_=src[w][:])
-                else:
-                    nc.scalar.sqrt(out=norm[w][:, j:j + 1], in_=src[w][:, j:j + 1])
-            nc.vector.reciprocal(out=rnorm[w][:], in_=norm[w][:])
-            nc.vector.tensor_tensor(out=row_gain[w][:], in0=rnorm[w][:], in1=vec["g" + w][:], op=ALU.mult)
+        def scale(w, j):
+            src = ss_act if on_scalar(w, j) else ss_dve
+            nc.scalar.activation(out=rnorm[w][:, j:j + 1], in_=src[w][:, j:j + 1], func=ACTF.Abs_reciprocal_sqrt)
 
         def mult(w, j):
             cols = slice(j * E, (j + 1) * E)
-            nc.vector.tensor_scalar(out=w_sb[w][:, cols], in0=v_raw[w][:, cols],
-                                    scalar1=row_gain[w][:, j:j + 1], scalar2=None, op0=ALU.mult)
+            nc.vector.tensor_scalar(out=w_sb[w][:, cols], in0=v_raw[w][:, cols], scalar1=rnorm[w][:, j:j + 1],
+                                    scalar2=gain[w][:, j:j + 1], op0=ALU.mult, op1=ALU.mult)
 
         def w_t(w, j, engine):
             w_grouped[(w, j)] = wgp.tile([P, E], BF16, name="w_grouped", align_bytes=64)
@@ -163,22 +156,23 @@ def tile_singleheadattention_pa_t_kernel(tc, query, key, Vq, gq, bq, Vk, gk, bk,
                                   in_=w_grouped[(w, j)][:])
 
         def bias_prep():
-            nc.vector.tensor_copy(out=bias["k"][:], in_=vec["bk"][:])
-            nc.vector.tensor_scalar(out=bias["q"][:], in0=vec["bq"][:], scalar1=SCALE, scalar2=None, op0=ALU.mult)
+            for w in ("q", "k"):
+                nc.gpsimd.tensor_copy(out=gain[w][:], in_=vec["g" + w][:])
+            nc.gpsimd.tensor_copy(out=bias["k"][:], in_=vec["bk"][:])
+            nc.gpsimd.tensor_scalar(out=bias["q"][:], in0=vec["bq"][:], scalar1=SCALE, scalar2=None, op0=ALU.mult)
 
-        def sort_words(n, engine):
+        def sort_words(n, b, count, engine):
             if n not in x_sorted:
                 x_sorted[n] = xpp.tile([P, UB * (E // 2)], F32, name="x_sorted")
-            words = raw[n][:].bitcast(F32)
+            cols = slice(b * (E // 2), (b + count) * (E // 2))
+            dst = x_sorted[n][:, cols].rearrange("p (u q) -> p u q", u=2)
+            src = raw[n][:].bitcast(F32)[:, cols].rearrange("p (q u) -> p u q", u=2)
             if engine == "act":
-                cols = slice(0, SORTED * (E // 2))
-                nc.scalar.copy(out=x_sorted[n][:, cols].rearrange("p (u q) -> p u q", u=2),
-                               in_=words[:, cols].rearrange("p (q u) -> p u q", u=2))
+                nc.scalar.copy(out=dst, in_=src)
             else:
-                for b in range(SORTED, SORTED + SORTED_VECTOR):
-                    cols = slice(b * (E // 2), (b + 1) * (E // 2))
-                    nc.vector.tensor_copy(out=x_sorted[n][:, cols].rearrange("p (u q) -> p u q", u=2),
-                                          in_=words[:, cols].rearrange("p (q u) -> p u q", u=2))
+                nc.vector.tensor_copy(out=dst, in_=src)
+            for m in range(count):
+                plane[(n, b + m)] = [(b * 2 + u * count + m) * (E // 4) for u in range(2)]
 
         def x_t(n, b):
             if b == 0:
@@ -190,9 +184,8 @@ def tile_singleheadattention_pa_t_kernel(tc, query, key, Vq, gq, bq, Vk, gk, bk,
             for g in range(PASSES):
                 for u in range(2):
                     gu = 2 * g + u
-                    if n in x_sorted and b < SORTED + SORTED_VECTOR:
-                        col = (u * SORTED + b) * (row_words // 2) if b < SORTED else (2 * b + u) * (row_words // 2)
-                        col += g * P
+                    if (n, b) in plane:
+                        col = plane[(n, b)][u] + g * P
                         picked = x_sorted[n][:, col:col + P]
                     else:
                         col = b * row_words + g * 2 * P
@@ -225,6 +218,12 @@ def tile_singleheadattention_pa_t_kernel(tc, query, key, Vq, gq, bq, Vk, gk, bk,
                                         lhsT=w_codes[w][:, wcols].bitcast(FP8X4), lhsT_scale=w_scales[w][:, wcols],
                                         rhs=x_codes[n][:, xcols].bitcast(FP8X4), rhs_scale=x_scales[n][:, xcols],
                                         start=(g == 0), stop=(g == PASSES - 1))
+            if n == len(UNITS) - 1 and b in (1,):
+                for j in range(PACK):
+                    nc.scalar.activation(out=q_grouped[n][:, b * P * PACK:(b + 1) * P * PACK].rearrange("c (r j) -> c j r", j=PACK)[:, j, :],
+                                         in_=bank[:, j * P:(j + 1) * P], func=ACTF.Identity, bias=bias[w][:, j:j + 1],
+                                         scale=post_scale[w])
+                return
             nc.vector.scalar_tensor_tensor(
                 out=q_grouped[n][:, b * P * PACK:(b + 1) * P * PACK].rearrange("c (r j) -> c r j", j=PACK),
                 in0=bank[:].rearrange("c (j r) -> c r j", j=PACK), scalar=post_scale[w],
@@ -270,7 +269,7 @@ def tile_singleheadattention_pa_t_kernel(tc, query, key, Vq, gq, bq, Vk, gk, bk,
                         load(n + RAW_BUFS)
 
         def tile_q(count):
-            if done["q"] < n_tiles:
+            if count and done["q"] < n_tiles:
                 x_q(done["q"] // UB, done["q"] % UB, count)
                 done["q"] += count
 
@@ -281,50 +280,65 @@ def tile_singleheadattention_pa_t_kernel(tc, query, key, Vq, gq, bq, Vk, gk, bk,
         for n in range(2, RAW_BUFS):
             load(n)
         warm(8)
-        tile_t(0)
+        bias_prep()
         for j in range(PACK):
             square("q", j)
-        bias_prep()
-        scale("q")
+            if j == 1:
+                scale("q", 0)
+            if j == 2:
+                scale("q", 1)
+        scale("q", 2)
+        scale("q", 3)
         tile_t(2)
         for j in range(PACK):
             mult("q", j)
         for j in range(PACK):
-            w_t("q", j, ("act", "dve")[j % 2])
+            w_t("q", j, "act")
             if j > 0:
-                w_q("q", j - 1)
+                w_q("q", j - 1 - 0)
         tile_q(2)
-        w_q("q", PACK - 1)
+        for j in range(PACK - 1 - 0, PACK):
+            w_q("q", j)
         tile_t(2)
-        key_steps = {1: [lambda: square("k", 0)], 3: [lambda: square("k", 1)], 5: [lambda: square("k", 2)], 7: [lambda: square("k", 3)], 9: [lambda: scale("k")], 10: [lambda: mult("k", 0)], 11: [lambda: mult("k", 1)], 12: [lambda: mult("k", 2)], 13: [lambda: mult("k", 3)], 14: [lambda: w_t("k", 0, "act"), lambda: w_t("k", 1, "act")], 16: [lambda: w_q("k", 0)], 17: [lambda: w_q("k", 1)], 18: [lambda: w_t("k", 2, "act"), lambda: w_t("k", 3, "act")], 20: [lambda: w_q("k", 2)], 21: [lambda: w_q("k", 3)]}
+        key_steps = {1: [lambda: square("k", 0)], 3: [lambda: square("k", 1)], 5: [lambda: square("k", 2)], 7: [lambda: square("k", 3)], 9: [lambda: (scale("k", 0), scale("k", 1), scale("k", 2), scale("k", 3))], 10: [lambda: mult("k", 0)], 11: [lambda: mult("k", 1)], 12: [lambda: mult("k", 2)], 13: [lambda: mult("k", 3)], 14: [lambda: w_t("k", 0, "act"), lambda: w_t("k", 1, "act")], 16: [lambda: w_q("k", 0)], 17: [lambda: w_q("k", 1)], 18: [lambda: w_t("k", 2, "act"), lambda: w_t("k", 3, "act")], 20: [lambda: w_q("k", 2)], 21: [lambda: w_q("k", 3)]}
         waiting = []
+        T_PLAN = (2,0,2,0,)
+        S_SORT = (0,2,0,0,)
+        V_SORT = (0,0,0,0,)
+        X_PLAN = (2,0,2,0,)
+        Q_PLAN = (None,(-1,2,2,),None,(0,0,2,),)
+        sorted_to = {}
         for i in range(n_units + 1):
             if 0 < i < n_units and UNITS[i - 1][0] == "q":
                 waiting.append(i - 1)
             for b in range(UB):
                 s = UB * i + b
-                if b % RUN == 0:
-                    tile_t(RUN)
-                    if s // RUN % 2 == 2 - 1 and done["t"] < s + RUN + T_AHEAD:
-                        tile_t(RUN)
+                if T_PLAN[b]:
+                    tile_t(T_PLAN[b])
+                    if s // 2 % 2 == 2 - 1 and done["t"] < s + 2 + T_AHEAD:
+                        tile_t(T_PLAN[b])
                 n = -(-done["t"] // UB)
-                if b == 1 and FIRST_SORT <= i and n < n_units and SORTED:
-                    sort_words(n, "act")
+                can_sort = FIRST_SORT <= i and n < n_units
+                first = sorted_to.get(n, 0)
+                if S_SORT[b] and can_sort and first + S_SORT[b] <= UB and done["t"] <= n * UB:
+                    sort_words(n, first, S_SORT[b], "act")
+                    first += S_SORT[b]
+                    sorted_to[n] = first
                 for step in key_steps.get(s, []):
                     step()
                 if i < n_units:
                     proj(i, b)
-                if b == 1 and FIRST_SORT <= i and n < n_units and SORTED_VECTOR:
-                    sort_words(n, "dve")
-                if b % 2 == 0:
-                    tile_q(2)
+                if V_SORT[b] and can_sort and first < UB and done["t"] <= n * UB:
+                    sort_words(n, first, V_SORT[b], "dve")
+                    sorted_to[n] = first + V_SORT[b]
+                if X_PLAN[b]:
+                    tile_q(X_PLAN[b])
                     if s % 4 == 4 - 2 and done["q"] < s + 2 + Q_AHEAD:
-                        tile_q(2)
-                elif i < n_units or b < 2:
-                    if b == 1 and i > 0:
-                        q_q(i - 1, 2, 2)
-                    if b == 3:
-                        q_q(i, 0, 2)
+                        tile_q(X_PLAN[b])
+                if Q_PLAN[b]:
+                    di, q_first, count = Q_PLAN[b]
+                    if 0 <= i + di < n_units:
+                        q_q(i + di, q_first, count)
                 if i >= KEY_AT + HALVES and i < n_units and (b == 3 or b == 1 and len(waiting) > 1) and waiting:
                     logits(waiting.pop(0), 0, UB)
         for n in waiting:

@@ -29,7 +29,7 @@ FIRST_SORT = 3
 ON_SCALAR = {"q": (0, 2,), "k": (0, 1, 2, 3,)}
 RUN = 2
 T_AHEAD = 8
-Q_AHEAD = 6
+Q_AHEAD = 8
 RAW_BUFS = 6
 
 
@@ -218,7 +218,7 @@ def tile_singleheadattention_pa_t_kernel(tc, query, key, Vq, gq, bq, Vk, gk, bk,
                                         lhsT=w_codes[w][:, wcols].bitcast(FP8X4), lhsT_scale=w_scales[w][:, wcols],
                                         rhs=x_codes[n][:, xcols].bitcast(FP8X4), rhs_scale=x_scales[n][:, xcols],
                                         start=(g == 0), stop=(g == PASSES - 1))
-            if n == len(UNITS) - 1 and b in (1,):
+            if (n - len(UNITS), b) in ((-2, 1), (-1, 0),):
                 for j in range(PACK):
                     nc.scalar.activation(out=q_grouped[n][:, b * P * PACK:(b + 1) * P * PACK].rearrange("c (r j) -> c j r", j=PACK)[:, j, :],
                                          in_=bank[:, j * P:(j + 1) * P], func=ACTF.Identity, bias=bias[w][:, j:j + 1],
@@ -300,11 +300,11 @@ def tile_singleheadattention_pa_t_kernel(tc, query, key, Vq, gq, bq, Vk, gk, bk,
         for j in range(PACK - 1 - 0, PACK):
             w_q("q", j)
         tile_t(2)
-        key_steps = {1: [lambda: square("k", 0)], 3: [lambda: square("k", 1)], 5: [lambda: square("k", 2)], 7: [lambda: square("k", 3)], 9: [lambda: (scale("k", 0), scale("k", 1), scale("k", 2), scale("k", 3))], 10: [lambda: mult("k", 0)], 11: [lambda: mult("k", 1)], 12: [lambda: mult("k", 2)], 13: [lambda: mult("k", 3)], 14: [lambda: w_t("k", 0, "act"), lambda: w_t("k", 1, "act")], 16: [lambda: w_q("k", 0)], 17: [lambda: w_q("k", 1)], 18: [lambda: w_t("k", 2, "act"), lambda: w_t("k", 3, "act")], 20: [lambda: w_q("k", 2)], 21: [lambda: w_q("k", 3)]}
+        key_steps = {1: [lambda: square("k", 0)], 3: [lambda: square("k", 1)], 5: [lambda: square("k", 2)], 7: [lambda: square("k", 3)], 9: [lambda: (scale("k", 0), scale("k", 1), scale("k", 2), scale("k", 3))], 10: [lambda: mult("k", 0)], 11: [lambda: mult("k", 1)], 12: [lambda: mult("k", 2)], 13: [lambda: mult("k", 3)], 15: [lambda: w_t("k", 0, "act"), lambda: w_t("k", 1, "act")], 17: [lambda: w_q("k", 0)], 18: [lambda: w_q("k", 1)], 19: [lambda: w_t("k", 2, "act"), lambda: w_t("k", 3, "act")], 21: [lambda: w_q("k", 2)], 22: [lambda: w_q("k", 3)]}
         waiting = []
         T_PLAN = (2,0,2,0,)
-        S_SORT = (0,2,0,0,)
-        V_SORT = (0,0,0,0,)
+        S_SORT = (0,2,0,0,0,2,0,0,)
+        V_SORT = (0,0,0,0,0,0,0,0,)
         X_PLAN = (2,0,2,0,)
         Q_PLAN = (None,(-1,2,2,),None,(0,0,2,),)
         sorted_to = {}
@@ -315,22 +315,22 @@ def tile_singleheadattention_pa_t_kernel(tc, query, key, Vq, gq, bq, Vk, gk, bk,
                 s = UB * i + b
                 if T_PLAN[b]:
                     tile_t(T_PLAN[b])
-                    if s // 2 % 2 == 2 - 1 and done["t"] < s + 2 + T_AHEAD:
-                        tile_t(T_PLAN[b])
+                elif b == 3 and i % 1 == 0 and done["t"] < s + 1 + T_AHEAD:
+                    tile_t(2)
                 n = -(-done["t"] // UB)
-                can_sort = FIRST_SORT <= i and n < n_units
+                can_sort = FIRST_SORT <= i < 99 and n < n_units
                 first = sorted_to.get(n, 0)
-                if S_SORT[b] and can_sort and first + S_SORT[b] <= UB and done["t"] <= n * UB:
-                    sort_words(n, first, S_SORT[b], "act")
-                    first += S_SORT[b]
+                if S_SORT[i % 2 * UB + b] and can_sort and first + S_SORT[i % 2 * UB + b] <= UB and done["t"] <= n * UB:
+                    sort_words(n, first, S_SORT[i % 2 * UB + b], "act")
+                    first += S_SORT[i % 2 * UB + b]
                     sorted_to[n] = first
                 for step in key_steps.get(s, []):
                     step()
                 if i < n_units:
                     proj(i, b)
-                if V_SORT[b] and can_sort and first < UB and done["t"] <= n * UB:
-                    sort_words(n, first, V_SORT[b], "dve")
-                    sorted_to[n] = first + V_SORT[b]
+                if V_SORT[i % 2 * UB + b] and 0 <= i < 99 and n < n_units and first < UB and done["t"] <= n * UB:
+                    sort_words(n, first, V_SORT[i % 2 * UB + b], "dve")
+                    sorted_to[n] = first + V_SORT[i % 2 * UB + b]
                 if X_PLAN[b]:
                     tile_q(X_PLAN[b])
                     if s % 4 == 4 - 2 and done["q"] < s + 2 + Q_AHEAD:

@@ -29,7 +29,7 @@ FIRST_SORT = 3
 ON_SCALAR = {"q": (0, 2,), "k": (0, 1, 2, 3,)}
 RUN = 2
 T_AHEAD = 8
-Q_AHEAD = 8
+Q_AHEAD = 6
 RAW_BUFS = 6
 
 
@@ -128,7 +128,8 @@ def tile_singleheadattention_pa_t_kernel(tc, query, key, Vq, gq, bq, Vk, gk, bk,
 
         def mult(w, j):
             cols = slice(j * E, (j + 1) * E)
-            nc.vector.tensor_scalar(out=w_sb[w][:, cols], in0=v_raw[w][:, cols], scalar1=rnorm[w][:, j:j + 1],
+            nc.vector.tensor_scalar(out=w_sb[w][:, cols].rearrange("c (u q h) -> c u q h", u=2, h=2),
+                                    in0=v_raw[w][:, cols].rearrange("c (q u h) -> c u q h", u=2, h=2), scalar1=rnorm[w][:, j:j + 1],
                                     scalar2=gain[w][:, j:j + 1], op0=ALU.mult, op1=ALU.mult)
 
         def w_t(w, j, engine):
@@ -140,8 +141,8 @@ def tile_singleheadattention_pa_t_kernel(tc, query, key, Vq, gq, bq, Vk, gk, bk,
             for g in range(PASSES):
                 for u in range(2):
                     gu = 2 * g + u
-                    col = j * row_words + g * 2 * P
-                    nc.tensor.transpose(out=bank[:, gu * P:(gu + 1) * P], in_=words_in[:, col + u:col + 2 * P:2],
+                    col = j * row_words + u * (row_words // 2) + g * P
+                    nc.tensor.transpose(out=bank[:, gu * P:(gu + 1) * P], in_=words_in[:, col:col + P],
                                         identity=ident_f[:])
             dst = words_out.rearrange("p (g c u) -> p g c u", g=PASSES, u=2)
             src = bank[:].rearrange("p (g u c) -> p g c u", g=PASSES, u=2)
@@ -218,7 +219,7 @@ def tile_singleheadattention_pa_t_kernel(tc, query, key, Vq, gq, bq, Vk, gk, bk,
                                         lhsT=w_codes[w][:, wcols].bitcast(FP8X4), lhsT_scale=w_scales[w][:, wcols],
                                         rhs=x_codes[n][:, xcols].bitcast(FP8X4), rhs_scale=x_scales[n][:, xcols],
                                         start=(g == 0), stop=(g == PASSES - 1))
-            if (n - len(UNITS), b) in ((-2, 1), (-1, 0),):
+            if (n - len(UNITS), b) in ((-3, 2), (-2, 1), (-1, 0)):
                 for j in range(PACK):
                     nc.scalar.activation(out=q_grouped[n][:, b * P * PACK:(b + 1) * P * PACK].rearrange("c (r j) -> c j r", j=PACK)[:, j, :],
                                          in_=bank[:, j * P:(j + 1) * P], func=ACTF.Identity, bias=bias[w][:, j:j + 1],
@@ -241,7 +242,7 @@ def tile_singleheadattention_pa_t_kernel(tc, query, key, Vq, gq, bq, Vk, gk, bk,
 
         def logits(n, first, count):
             c, h = divmod(UNITS[n][1], HALVES)
-            bank = ps_q.tile([P, UB * S], F32, name="l_bank", tag="q_bank")
+            bank = ps_t.tile([P, UB * S], F32, name="l_bank", tag="t_bank")
             for m in range(count):
                 qcols = slice((first + m) * P, (first + m + 1) * P)
                 kcols = slice((h * UB + first + m) * S, (h * UB + first + m + 1) * S)

from contextlib import ExitStack

import concourse.mybir as mybir
from concourse.masks import make_identity

F32 = mybir.dt.float32
BF16 = mybir.dt.bfloat16
U32 = mybir.dt.uint32
U8 = mybir.dt.uint8
FP8X4 = mybir.dt.float8_e4m3fn_x4
ALU = mybir.AluOpType
ACTF = mybir.ActivationFunctionType

T, S, B, E, H = 1024, 128, 8, 1024, 512
P = 128
PACK = 4
PASSES = E // (P * PACK)
SCALE = H ** -0.5
FLOPS = 2 * (T * B * E * H + S * B * E * H + B * T * S * H)

UB = 4
HALVES = B // UB
KEY_AT = 6
QUERIES = [("q", i) for i in range((T // P) * HALVES)]
UNITS = QUERIES[:KEY_AT] + [("k", h) for h in range(HALVES)] + QUERIES[KEY_AT:]
SORTED = 2
SORTED_VECTOR = 1
FIRST_SORT = 3
ON_SCALAR = {"q": (0, 2,), "k": (0, 1, 2, 3,)}
RUN = 2
T_AHEAD = 8
Q_AHEAD = 6
RAW_BUFS = 6


def tile_singleheadattention_pa_t_kernel(tc, query, key, Vq, gq, bq, Vk, gk, bk, out):
    nc = tc.nc
    with ExitStack() as ctx:
        const = ctx.enter_context(tc.tile_pool(name="const", bufs=1))
        rawp = ctx.enter_context(tc.tile_pool(name="rawp", bufs=RAW_BUFS))
        wgp = ctx.enter_context(tc.tile_pool(name="wgp", bufs=4))
        xgp = ctx.enter_context(tc.tile_pool(name="xgp", bufs=3))
        xcp = ctx.enter_context(tc.tile_pool(name="xcp", bufs=3))
        qgp = ctx.enter_context(tc.tile_pool(name="qgp", bufs=3))
        qcp = ctx.enter_context(tc.tile_pool(name="qcp", bufs=KEY_AT + 5))
        xpp = ctx.enter_context(tc.tile_pool(name="xpp", bufs=3))
        otp = ctx.enter_context(tc.tile_pool(name="otp", bufs=3))
        ps_t = ctx.enter_context(tc.psum_pool(name="ps_t", bufs=4))
        ps_q = ctx.enter_context(tc.psum_pool(name="ps_q", bufs=4))
        ctx.enter_context(tc.manual_schedule())

        vec = {}
        for nm, src in (("gk", gk), ("bk", bk), ("gq", gq), ("bq", bq)):
            vt = const.tile([P, PACK], BF16, name="vec_" + nm)
            nc.scalar.dma_start(out=vt[:], in_=src.rearrange("(c j) -> c j", j=PACK))
            vec[nm] = vt
        warm_in = const.tile([P, 1], F32, name="warm_in")
        warm_out = const.tile([P, 1], F32, name="warm_out")
        nc.vector.memset(warm_in[:], 1.0)
        nc.scalar.activation(out=warm_out[:], in_=warm_in[:], func=ACTF.Abs_reciprocal_sqrt)
        ident_b = const.tile([P, P], BF16, name="ident_b")
        ident_f = const.tile([P, P], F32, name="ident_f")
        make_identity(nc, ident_b[:])
        make_identity(nc, ident_f[:])

        warm_rhs = const.tile([P, PACK * P], BF16, name="warm_rhs")
        nc.vector.memset(warm_rhs[:], 0.0)

        def warm(count):
            bank = ps_q.tile([P, PACK * P], F32, name="warm_bank", tag="q_bank")
            for m in range(count):
                nc.tensor.matmul(out=bank[:], lhsT=ident_b[:], rhs=warm_rhs[:], start=True, stop=True)

        v_dram = {"q": Vq, "k": Vk}
        post_scale = {"q": SCALE, "k": 1.0}
        v_raw, w_sb, ss_act, ss_dve, rnorm, gain, w_codes, w_scales, bias = {}, {}, {}, {}, {}, {}, {}, {}, {}
        for w in ("k", "q"):
            v_raw[w] = const.tile([P, PACK * E], BF16, name="v_raw_" + w)
            w_sb[w] = const.tile([P, PACK * E], BF16, name="w_sb_" + w)
            ss_act[w] = const.tile([P, PACK], F32, name="ss_act_" + w)
            ss_dve[w] = const.tile([P, PACK], F32, name="ss_dve_" + w)
            rnorm[w] = const.tile([P, PACK], F32, name="rnorm_" + w)
            gain[w] = const.tile([P, PACK], F32, name="gain_" + w)
            bias[w] = const.tile([P, PACK], F32, name="bias_" + w)
            w_codes[w] = const.tile([P, PACK * PASSES * P], U32, name="w_codes_" + w, align_bytes=64)
            w_scales[w] = const.tile([P, PACK * PASSES * P], U8, name="w_scales_" + w, align_bytes=64)
        squares_act = const.tile([P, E], BF16, name="squares_act")
        squares_dve = const.tile([P, E], BF16, name="squares_dve")
        k_codes = const.tile([P, B * S], U32, name="k_codes", align_bytes=64)
        k_scales = const.tile([P, B * S], U8, name="k_scales", align_bytes=64)

        plane = {}
        raw, x_sorted, x_grouped, x_codes, x_scales, q_grouped, q_codes, q_scales, w_grouped = {}, {}, {}, {}, {}, {}, {}, {}, {}

        def load_v(w):
            src = v_dram[w].rearrange("(c j) e -> c j e", j=PACK)
            for j in range(PACK):
                nc.sync.dma_start(out=v_raw[w][:, j * E:(j + 1) * E], in_=src[:, j, :])

        def load(n):
            kind, i = UNITS[n]
            raw[n] = rawp.tile([P, UB * E], BF16, name="raw")
            if kind == "k":
                src = key[:, UB * i:UB * (i + 1), :]
            else:
                c, h = divmod(i, HALVES)
                src = query[P * c:P * (c + 1), UB * h:UB * (h + 1), :]
            pieces = UB if n == 0 else 1
            width = UB // pieces
            for m in range(pieces):
                nc.sync.dma_start(out=raw[n][:, m * width * E:(m + 1) * width * E],
                                  in_=src[:, m * width:(m + 1) * width, :].rearrange("t b e -> t (b e)"))

        def on_scalar(w, j):
            return j in ON_SCALAR[w]

        def square(w, j):
            vj = v_raw[w][:, j * E:(j + 1) * E]
            if on_scalar(w, j):
                nc.scalar.activation(out=squares_act[:], in_=vj, func=ACTF.Square, accum_out=ss_act[w][:, j:j + 1])
            else:
                nc.vector.scalar_tensor_tensor(out=squares_dve[:], in0=vj, scalar=1.0, in1=vj, op0=ALU.mult,
                                               op1=ALU.mult, accum_out=ss_dve[w][:, j:j + 1])

        def scale(w, j):
            src = ss_act if on_scalar(w, j) else ss_dve
            nc.scalar.activation(out=rnorm[w][:, j:j + 1], in_=src[w][:, j:j + 1], func=ACTF.Abs_reciprocal_sqrt)

        def mult(w, j):
            cols = slice(j * E, (j + 1) * E)
            nc.vector.tensor_scalar(out=w_sb[w][:, cols].rearrange("c (u q h) -> c u q h", u=2, h=2),
                                    in0=v_raw[w][:, cols].rearrange("c (q u h) -> c u q h", u=2, h=2), scalar1=rnorm[w][:, j:j + 1],
                                    scalar2=gain[w][:, j:j + 1], op0=ALU.mult, op1=ALU.mult)

        def w_t(w, j, engine):
            w_grouped[(w, j)] = wgp.tile([P, E], BF16, name="w_grouped", align_bytes=64)
            words_in = w_sb[w][:].bitcast(F32)
            words_out = w_grouped[(w, j)][:].bitcast(F32)
            row_words = E // 2
            bank = ps_t.tile([P, row_words], F32, name="w_bank", tag="t_bank")
            for g in range(PASSES):
                for u in range(2):
                    gu = 2 * g + u
                    col = j * row_words + u * (row_words // 2) + g * P
                    nc.tensor.transpose(out=bank[:, gu * P:(gu + 1) * P], in_=words_in[:, col:col + P],
                                        identity=ident_f[:])
            dst = words_out.rearrange("p (g c u) -> p g c u", g=PASSES, u=2)
            src = bank[:].rearrange("p (g u c) -> p g c u", g=PASSES, u=2)
            if engine == "act":
                nc.scalar.copy(out=dst, in_=src)
            else:
                nc.vector.tensor_copy(out=dst, in_=src)

        def w_q(w, j):
            cols = slice(j * PASSES * P, (j + 1) * PASSES * P)
            nc.vector.quantize_mx(out=w_codes[w][:, cols].bitcast(FP8X4), scales=w_scales[w][:, cols],
                                  in_=w_grouped[(w, j)][:])

        def bias_prep():
            for w in ("q", "k"):
                nc.gpsimd.tensor_copy(out=gain[w][:], in_=vec["g" + w][:])
            nc.gpsimd.tensor_copy(out=bias["k"][:], in_=vec["bk"][:])
            nc.gpsimd.tensor_scalar(out=bias["q"][:], in0=vec["bq"][:], scalar1=SCALE, scalar2=None, op0=ALU.mult)

        def sort_words(n, b, count, engine):
            if n not in x_sorted:
                x_sorted[n] = xpp.tile([P, UB * (E // 2)], F32, name="x_sorted")
            cols = slice(b * (E // 2), (b + count) * (E // 2))
            dst = x_sorted[n][:, cols].rearrange("p (u q) -> p u q", u=2)
            src = raw[n][:].bitcast(F32)[:, cols].rearrange("p (q u) -> p u q", u=2)
            if engine == "act":
                nc.scalar.copy(out=dst, in_=src)
            else:
                nc.vector.tensor_copy(out=dst, in_=src)
            for m in range(count):
                plane[(n, b + m)] = [(b * 2 + u * count + m) * (E // 4) for u in range(2)]

        def x_t(n, b):
            if b == 0:
                x_grouped[n] = xgp.tile([P, UB * E], BF16, name="x_grouped", align_bytes=64)
            words_in = raw[n][:].bitcast(F32)
            words_out = x_grouped[n][:].bitcast(F32)
            row_words = E // 2
            bank = ps_t.tile([P, row_words], F32, name="x_bank", tag="t_bank")
            for g in range(PASSES):
                for u in range(2):
                    gu = 2 * g + u
                    if (n, b) in plane:
                        col = plane[(n, b)][u] + g * P
                        picked = x_sorted[n][:, col:col + P]
                    else:
                        col = b * row_words + g * 2 * P
                        picked = words_in[:, col + u:col + 2 * P:2]
                    nc.tensor.transpose(out=bank[:, gu * P:(gu + 1) * P], in_=picked, identity=ident_f[:])
            dst = words_out[:, b * row_words:(b + 1) * row_words].rearrange("p (g r u) -> p g r u", g=PASSES, u=2)
            nc.scalar.copy(out=dst, in_=bank[:].rearrange("p (g u r) -> p g r u", g=PASSES, u=2))

        def x_q(n, b, count):
            if b == 0:
                x_codes[n] = xcp.tile([P, UB * PASSES * P], U32, name="x_codes", align_bytes=64)
                x_scales[n] = xcp.tile([P, UB * PASSES * P], U8, name="x_scales", align_bytes=64)
            cols = slice(b * PASSES * P, (b + count) * PASSES * P)
            nc.vector.quantize_mx(out=x_codes[n][:, cols].bitcast(FP8X4), scales=x_scales[n][:, cols],
                                  in_=x_grouped[n][:, b * E:(b + count) * E])

        def proj(n, b):
            w = UNITS[n][0]
            if b == 0:
                q_grouped[n] = qgp.tile([P, UB * P * PACK], BF16, name="q_grouped", align_bytes=64)
                if w == "q":
                    q_codes[n] = qcp.tile([P, UB * P], U32, name="q_codes", align_bytes=64)
                    q_scales[n] = qcp.tile([P, UB * P], U8, name="q_scales", align_bytes=64)
            bank = ps_q.tile([P, PACK * P], F32, name="q_bank", tag="q_bank")
            for j in range(PACK):
                for g in range(PASSES):
                    wcols = slice((j * PASSES + g) * P, (j * PASSES + g + 1) * P)
                    xcols = slice((b * PASSES + g) * P, (b * PASSES + g + 1) * P)
                    nc.tensor.matmul_mx(out=bank[:, j * P:(j + 1) * P],
                                        lhsT=w_codes[w][:, wcols].bitcast(FP8X4), lhsT_scale=w_scales[w][:, wcols],
                                        rhs=x_codes[n][:, xcols].bitcast(FP8X4), rhs_scale=x_scales[n][:, xcols],
                                        start=(g == 0), stop=(g == PASSES - 1))
            if (n - len(UNITS), b) in ((-3, 2), (-2, 1), (-1, 0)):
                for j in range(PACK):
                    nc.scalar.activation(out=q_grouped[n][:, b * P * PACK:(b + 1) * P * PACK].rearrange("c (r j) -> c j r", j=PACK)[:, j, :],
                                         in_=bank[:, j * P:(j + 1) * P], func=ACTF.Identity, bias=bias[w][:, j:j + 1],
                                         scale=post_scale[w])
                return
            nc.vector.scalar_tensor_tensor(
                out=q_grouped[n][:, b * P * PACK:(b + 1) * P * PACK].rearrange("c (r j) -> c r j", j=PACK),
                in0=bank[:].rearrange("c (j r) -> c r j", j=PACK), scalar=post_scale[w],
                in1=bias[w][:].unsqueeze(1).to_broadcast([P, P, PACK]), op0=ALU.mult, op1=ALU.add)

        def q_q(n, first, count):
            w, i = UNITS[n]
            src = q_grouped[n][:, first * P * PACK:(first + count) * P * PACK]
            if w == "k":
                cols = slice((i * UB + first) * P, (i * UB + first + count) * P)
                nc.vector.quantize_mx(out=k_codes[:, cols].bitcast(FP8X4), scales=k_scales[:, cols], in_=src)
            else:
                cols = slice(first * P, (first + count) * P)
                nc.vector.quantize_mx(out=q_codes[n][:, cols].bitcast(FP8X4), scales=q_scales[n][:, cols], in_=src)

        def logits(n, first, count):
            c, h = divmod(UNITS[n][1], HALVES)
            bank = ps_t.tile([P, UB * S], F32, name="l_bank", tag="t_bank")
            for m in range(count):
                qcols = slice((first + m) * P, (first + m + 1) * P)
                kcols = slice((h * UB + first + m) * S, (h * UB + first + m + 1) * S)
                nc.tensor.matmul_mx(out=bank[:, m * S:(m + 1) * S],
                                    lhsT=q_codes[n][:, qcols].bitcast(FP8X4), lhsT_scale=q_scales[n][:, qcols],
                                    rhs=k_codes[:, kcols].bitcast(FP8X4), rhs_scale=k_scales[:, kcols],
                                    start=True, stop=True)
            staged = otp.tile([P, UB * S], F32, name="staged")
            nc.scalar.copy(out=staged[:, :count * S], in_=bank[:, :count * S])
            batches = slice(UB * h + first, UB * h + first + count)
            nc.sync.dma_start(out=out[batches, P * c:P * (c + 1), :].rearrange("b t s -> t b s"),
                                in_=staged[:, :count * S].rearrange("t (b s) -> t b s", b=count))

        n_units = len(UNITS)
        n_tiles = n_units * UB
        done = {"t": 0, "q": 0}

        def tile_t(count):
            for m in range(count):
                if done["t"] < n_tiles:
                    n, b = divmod(done["t"], UB)
                    x_t(n, b)
                    done["t"] += 1
                    if b == UB - 1 and n + RAW_BUFS < n_units:
                        load(n + RAW_BUFS)

        def tile_q(count):
            if count and done["q"] < n_tiles:
                x_q(done["q"] // UB, done["q"] % UB, count)
                done["q"] += count

        load_v("q")
        load(0)
        load(1)
        load_v("k")
        for n in range(2, RAW_BUFS):
            load(n)
        warm(8)
        bias_prep()
        for j in range(PACK):
            square("q", j)
            if j == 1:
                scale("q", 0)
            if j == 2:
                scale("q", 1)
        scale("q", 2)
        scale("q", 3)
        tile_t(2)
        for j in range(PACK):
            mult("q", j)
        for j in range(PACK):
            w_t("q", j, "act")
            if j > 0:
                w_q("q", j - 1 - 0)
        tile_q(2)
        for j in range(PACK - 1 - 0, PACK):
            w_q("q", j)
        tile_t(2)
        key_steps = {1: [lambda: square("k", 0)], 3: [lambda: square("k", 1)], 5: [lambda: square("k", 2)], 7: [lambda: square("k", 3)], 9: [lambda: (scale("k", 0), scale("k", 1), scale("k", 2), scale("k", 3))], 10: [lambda: mult("k", 0)], 11: [lambda: mult("k", 1)], 12: [lambda: mult("k", 2)], 13: [lambda: mult("k", 3)], 15: [lambda: w_t("k", 0, "act"), lambda: w_t("k", 1, "act")], 17: [lambda: w_q("k", 0)], 18: [lambda: w_q("k", 1)], 19: [lambda: w_t("k", 2, "act"), lambda: w_t("k", 3, "act")], 21: [lambda: w_q("k", 2)], 22: [lambda: w_q("k", 3)]}
        waiting = []
        T_PLAN = (2,0,2,0,)
        S_SORT = (0,2,0,0,0,2,0,0,)
        V_SORT = (0,0,0,0,0,0,0,0,)
        X_PLAN = (2,0,2,0,)
        Q_PLAN = (None,(-1,2,2,),None,(0,0,2,),)
        sorted_to = {}
        for i in range(n_units + 1):
            if 0 < i < n_units and UNITS[i - 1][0] == "q":
                waiting.append(i - 1)
            for b in range(UB):
                s = UB * i + b
                if T_PLAN[b]:
                    tile_t(T_PLAN[b])
                elif b == 3 and i % 1 == 0 and done["t"] < s + 1 + T_AHEAD:
                    tile_t(2)
                n = -(-done["t"] // UB)
                can_sort = FIRST_SORT <= i < 99 and n < n_units
                first = sorted_to.get(n, 0)
                if S_SORT[i % 2 * UB + b] and can_sort and first + S_SORT[i % 2 * UB + b] <= UB and done["t"] <= n * UB:
                    sort_words(n, first, S_SORT[i % 2 * UB + b], "act")
                    first += S_SORT[i % 2 * UB + b]
                    sorted_to[n] = first
                for step in key_steps.get(s, []):
                    step()
                if i < n_units:
                    proj(i, b)
                if V_SORT[i % 2 * UB + b] and 0 <= i < 99 and n < n_units and first < UB and done["t"] <= n * UB:
                    sort_words(n, first, V_SORT[i % 2 * UB + b], "dve")
                    sorted_to[n] = first + V_SORT[i % 2 * UB + b]
                if X_PLAN[b]:
                    tile_q(X_PLAN[b])
                    if s % 4 == 4 - 2 and done["q"] < s + 2 + Q_AHEAD:
                        tile_q(X_PLAN[b])
                if Q_PLAN[b]:
                    di, q_first, count = Q_PLAN[b]
                    if 0 <= i + di < n_units:
                        q_q(i + di, q_first, count)
                if i >= KEY_AT + HALVES and i < n_units and (b == 3 or b == 1 and len(waiting) > 1) and waiting:
                    logits(waiting.pop(0), 0, UB)
        for n in waiting:
            logits(n, 0, UB)
        logits(n_units - 1, 0, 2)
        logits(n_units - 1, 2, 2)
